import numpy as np
import ml_dtypes


def mxq(x, axis, fmt="e4m3"):
    dtype, down = {"e4m3": (ml_dtypes.float8_e4m3fn, 7), "e5m2": (ml_dtypes.float8_e5m2, 14)}[fmt]
    v = np.moveaxis(np.asarray(x, np.float32).astype(ml_dtypes.bfloat16).astype(np.float64), axis, -1)
    blocks = v.reshape(v.shape[:-1] + (-1, 32))
    amax = np.abs(blocks).max(-1, keepdims=True)
    byte = np.maximum(np.where(amax > 0, np.frexp(amax)[1] - 1 + 127, 0) - down, 1)
    scale = np.exp2(byte - 127.0)
    codes = (blocks / scale).astype(np.float32).astype(dtype).astype(np.float64)
    return np.moveaxis((codes * scale).reshape(v.shape), -1, axis)


WIDE = False


def mx_kscale(k):
    if not WIDE:
        return np.ones(k)
    levels = np.array([10, -10, 5, -5, 0])
    a = np.random.permutation(np.resize(levels, k // 512 * 4)).reshape(k // 512, 4)
    idx = np.arange(k)
    return np.exp2(a[idx // 512, idx % 128 // 32])


BF16 = ml_dtypes.bfloat16


def bf(x):
    return np.asarray(x, np.float32).astype(BF16)


def f64(x):
    return np.asarray(x).astype(np.float64)


T, K, E, H, KVH, D = 8192, 1024, 1024, 2, 4, 64
EPS = 1e-05


def rmsnorm(x, w):
    var = np.mean(np.square(x), axis=-1, keepdims=True)
    return x * (1.0 / np.sqrt(var + EPS)) * w


def setup_inputs():
    s = mx_kscale(E)
    return {"hidden_states": bf(np.random.standard_normal((T, E)) * s),
            "Wq": bf(np.random.standard_normal((H * D, E)) / np.sqrt(E) / s),
            "q_norm_w": bf(1.5 + 0.1 * np.random.standard_normal(D))}


def reference(hidden_states, Wq, q_norm_w):
    q = mxq(f64(hidden_states), 1, "e4m3") @ mxq(f64(Wq), 1, "e4m3").T
    qh = rmsnorm(q.reshape(T, H, D), f64(q_norm_w))
    return qh.transpose(1, 0, 2)

@@ -1,0 +1,147 @@
+import math
+from contextlib import ExitStack
+
+import concourse.mybir as mybir
+from concourse.masks import make_identity
+
+F32 = mybir.dt.float32
+BF16 = mybir.dt.bfloat16
+U32 = mybir.dt.uint32
+U8 = mybir.dt.uint8
+FP8X4 = mybir.dt.float8_e4m3fn_x4
+ACT = mybir.ActivationFunctionType
+ALU = mybir.AluOpType
+
+T, E, H, D = 8192, 1024, 2, 64
+EPS = 1e-05
+FLOPS = 2 * T * E * H * D
+
+P = 128
+PACK = 4
+K_PASS = P * PACK
+PASSES = E // K_PASS
+HALVES = 2
+TILES = 4
+CHUNK_ROWS = TILES * P
+CHUNKS = T // CHUNK_ROWS
+VECTOR_TILE = TILES - 1
+
+
+def tile_combcrossattention_pa_t_kernel(tc, hidden_states, Wq, q_norm_w, out):
+    nc = tc.nc
+    x_view = hidden_states.rearrange("(c p j) k -> c p j k", p=P, j=TILES)
+    out_view = out.rearrange("h (c p j) d -> c p h (j d)", p=P, j=TILES)
+
+    with ExitStack() as ctx:
+        const = ctx.enter_context(tc.tile_pool(name="const", bufs=1))
+        resident = ctx.enter_context(tc.tile_pool(name="resident", bufs=1))
+        group_pool = ctx.enter_context(tc.tile_pool(name="group", bufs=2 * TILES))
+        mx_pool = ctx.enter_context(tc.tile_pool(name="mx", bufs=2 * TILES))
+        stat_pool = ctx.enter_context(tc.tile_pool(name="stat", bufs=3))
+        out_pool = ctx.enter_context(tc.tile_pool(name="outp", bufs=4))
+        flip_psum = ctx.enter_context(tc.psum_pool(name="flip", bufs=6))
+        q_psum = ctx.enter_context(tc.psum_pool(name="q", bufs=2))
+        ctx.enter_context(tc.manual_schedule())
+
+        def transpose_rows(rows):
+            words = rows.bitcast(F32)
+            flipped = flip_psum.tile([P, PASSES, HALVES, P], F32)
+            for g in range(PASSES):
+                for u in range(HALVES):
+                    first = (g * HALVES + u) * P
+                    nc.tensor.transpose(flipped[:, g, u, :], words[:, first : first + P], ident[:])
+            return flipped
+
+        def regroup(copy, flipped):
+            grouped = group_pool.tile([P, PASSES, P, PACK], BF16, align_bytes=64)
+            copy(out=grouped[:].bitcast(F32), in_=flipped[:].rearrange("p g u r -> p g r u"))
+            return grouped
+
+        def quantise(grouped, pool):
+            codes = pool.tile([P, PASSES * P], U32, align_bytes=64)
+            scales = pool.tile([P, PASSES * P], U8, align_bytes=64)
+            nc.vector.quantize_mx(
+                out=codes[:].bitcast(FP8X4),
+                scales=scales[:],
+                in_=grouped[:].rearrange("p g r e -> p (g r e)"),
+            )
+            return codes, scales
+
+        def project(x_mx):
+            q = q_psum.tile([P, TILES, H * D], F32)
+            for j in range(TILES):
+                codes, scales = x_mx[j]
+                for g in range(PASSES):
+                    cols = slice(g * P, (g + 1) * P)
+                    nc.tensor.matmul_mx(
+                        out=q[:, j, :],
+                        lhsT=codes[:, cols].bitcast(FP8X4),
+                        lhsT_scale=scales[:, cols],
+                        rhs=w_codes[:, cols].bitcast(FP8X4),
+                        rhs_scale=w_scales[:, cols],
+                        start=(g == 0),
+                        stop=(g == PASSES - 1),
+                    )
+            return q
+
+        def inverse_rms(q):
+            squares = stat_pool.tile([P, TILES, H, D], F32)
+            mean_sq = stat_pool.tile([P, TILES, H], F32)
+            for j in range(TILES):
+                for h in range(H):
+                    nc.scalar.activation(
+                        out=squares[:, j, h, :],
+                        in_=q[:, j, h * D : (h + 1) * D],
+                        func=ACT.Square,
+                        scale=1.0 / math.sqrt(D),
+                        accum_out=mean_sq[:, j, h : h + 1],
+                    )
+            rstd = stat_pool.tile([P, TILES, H], F32)
+            nc.scalar.activation(out=rstd[:], in_=mean_sq[:], func=ACT.Abs_reciprocal_sqrt, bias=eps[:])
+            return rstd
+
+        def normalise_and_store(c, q, rstd):
+            normed = out_pool.tile([P, H, TILES, D], F32)
+            for j in range(TILES):
+                for h in range(H):
+                    nc.vector.scalar_tensor_tensor(
+                        out=normed[:, h, j, :],
+                        in0=q[:, j, h * D : (h + 1) * D],
+                        scalar=rstd[:, j, h : h + 1],
+                        in1=gain[:],
+                        op0=ALU.mult,
+                        op1=ALU.mult,
+                    )
+            nc.gpsimd.dma_start(out=out_view[c], in_=normed[:].rearrange("p h j d -> p h (j d)"))
+
+        ident = const.tile([P, P], F32)
+        make_identity(nc, ident[:])
+        eps = const.tile([P, 1], F32)
+        nc.vector.memset(eps[:], EPS)
+        gain = const.tile([P, D], BF16)
+        nc.scalar.dma_start(out=gain[:], in_=q_norm_w.partition_broadcast(P))
+        w_rows = const.tile([P, E], BF16)
+        nc.sync.dma_start(out=w_rows[:], in_=Wq)
+        x_rows = []
+        for c in range(CHUNKS):
+            x_chunk = resident.tile([P, TILES, E], BF16, name="x%d" % c)
+            nc.sync.dma_start(out=x_chunk[:], in_=x_view[c])
+            x_rows.append(x_chunk)
+
+        w_codes, w_scales = quantise(regroup(nc.vector.tensor_copy, transpose_rows(w_rows[:])), const)
+
+        x_mx = None
+        for i in range(CHUNKS + 1):
+            if i < CHUNKS:
+                flipped = [transpose_rows(x_rows[i][:, j, :]) for j in range(TILES)]
+            if i > 0:
+                q = project(x_mx)
+            if i < CHUNKS:
+                grouped = [None] * TILES
+                for j in range(TILES):
+                    copy = nc.vector.tensor_copy if j == VECTOR_TILE else nc.scalar.copy
+                    grouped[j] = regroup(copy, flipped[j])
+                x_mx = [quantise(grouped[j], mx_pool) for j in range(TILES)]
+            if i > 0:
+                rstd = inverse_rms(q)
+                normalise_and_store(i - 1, q, rstd)

@@ -24,6 +24,7 @@ HALVES = 2
 TILES = 4
 CHUNK_ROWS = TILES * P
 CHUNKS = T // CHUNK_ROWS
+SPARE_PASSES = 4
 VECTOR_TILE = TILES - 1
 
 
@@ -39,7 +40,8 @@ def tile_combcrossattention_pa_t_kernel(tc, hidden_states, Wq, q_norm_w, out):
         mx_pool = ctx.enter_context(tc.tile_pool(name="mx", bufs=2 * TILES))
         stat_pool = ctx.enter_context(tc.tile_pool(name="stat", bufs=3))
         out_pool = ctx.enter_context(tc.tile_pool(name="outp", bufs=4))
-        flip_psum = ctx.enter_context(tc.psum_pool(name="flip", bufs=6))
+        flip_psum = ctx.enter_context(tc.psum_pool(name="flip", bufs=5))
+        spare_psum = ctx.enter_context(tc.psum_pool(name="spare", bufs=1))
         q_psum = ctx.enter_context(tc.psum_pool(name="q", bufs=2))
         ctx.enter_context(tc.manual_schedule())
 
@@ -83,6 +85,18 @@ def tile_combcrossattention_pa_t_kernel(tc, hidden_states, Wq, q_norm_w, out):
                         stop=(g == PASSES - 1),
                     )
             return q
+
+        def hold_clock():
+            for n in range(SPARE_PASSES):
+                nc.tensor.matmul_mx(
+                    out=spare[:],
+                    lhsT=w_codes[:, 0:P].bitcast(FP8X4),
+                    lhsT_scale=w_scales[:, 0:P],
+                    rhs=w_codes[:].bitcast(FP8X4),
+                    rhs_scale=w_scales[:],
+                    start=True,
+                    stop=True,
+                )
 
         def inverse_rms(q):
             squares = stat_pool.tile([P, TILES, H, D], F32)
@@ -130,12 +144,14 @@ def tile_combcrossattention_pa_t_kernel(tc, hidden_states, Wq, q_norm_w, out):
 
         w_codes, w_scales = quantise(regroup(nc.vector.tensor_copy, transpose_rows(w_rows[:])), const)
 
+        spare = spare_psum.tile([P, PASSES * P], F32)
         x_mx = None
         for i in range(CHUNKS + 1):
             if i < CHUNKS:
                 flipped = [transpose_rows(x_rows[i][:, j, :]) for j in range(TILES)]
             if i > 0:
                 q = project(x_mx)
+                hold_clock()
             if i < CHUNKS:
                 grouped = [None] * TILES
                 for j in range(TILES):

@@ -24,7 +24,6 @@ HALVES = 2
 TILES = 4
 CHUNK_ROWS = TILES * P
 CHUNKS = T // CHUNK_ROWS
-SPARE_PASSES = 4
 VECTOR_TILE = TILES - 1
 
 
@@ -39,9 +38,8 @@ def tile_combcrossattention_pa_t_kernel(tc, hidden_states, Wq, q_norm_w, out):
         group_pool = ctx.enter_context(tc.tile_pool(name="group", bufs=2 * TILES))
         mx_pool = ctx.enter_context(tc.tile_pool(name="mx", bufs=2 * TILES))
         stat_pool = ctx.enter_context(tc.tile_pool(name="stat", bufs=3))
-        out_pool = ctx.enter_context(tc.tile_pool(name="outp", bufs=4))
-        flip_psum = ctx.enter_context(tc.psum_pool(name="flip", bufs=5))
-        spare_psum = ctx.enter_context(tc.psum_pool(name="spare", bufs=1))
+        out_pool = ctx.enter_context(tc.tile_pool(name="outp", bufs=CHUNKS))
+        flip_psum = ctx.enter_context(tc.psum_pool(name="flip", bufs=6))
         q_psum = ctx.enter_context(tc.psum_pool(name="q", bufs=2))
         ctx.enter_context(tc.manual_schedule())
 
@@ -86,18 +84,6 @@ def tile_combcrossattention_pa_t_kernel(tc, hidden_states, Wq, q_norm_w, out):
                     )
             return q
 
-        def hold_clock():
-            for n in range(SPARE_PASSES):
-                nc.tensor.matmul_mx(
-                    out=spare[:],
-                    lhsT=w_codes[:, 0:P].bitcast(FP8X4),
-                    lhsT_scale=w_scales[:, 0:P],
-                    rhs=w_codes[:].bitcast(FP8X4),
-                    rhs_scale=w_scales[:],
-                    start=True,
-                    stop=True,
-                )
-
         def inverse_rms(q):
             squares = stat_pool.tile([P, TILES, H, D], F32)
             mean_sq = stat_pool.tile([P, TILES, H], F32)
@@ -126,7 +112,7 @@ def tile_combcrossattention_pa_t_kernel(tc, hidden_states, Wq, q_norm_w, out):
                         op0=ALU.mult,
                         op1=ALU.mult,
                     )
-            nc.gpsimd.dma_start(out=out_view[c], in_=normed[:].rearrange("p h j d -> p h (j d)"))
+            nc.sync.dma_start(out=out_view[c], in_=normed[:].rearrange("p h j d -> p h (j d)"))
 
         ident = const.tile([P, P], F32)
         make_identity(nc, ident[:])
@@ -144,14 +130,12 @@ def tile_combcrossattention_pa_t_kernel(tc, hidden_states, Wq, q_norm_w, out):
 
         w_codes, w_scales = quantise(regroup(nc.vector.tensor_copy, transpose_rows(w_rows[:])), const)
 
-        spare = spare_psum.tile([P, PASSES * P], F32)
         x_mx = None
         for i in range(CHUNKS + 1):
             if i < CHUNKS:
                 flipped = [transpose_rows(x_rows[i][:, j, :]) for j in range(TILES)]
             if i > 0:
                 q = project(x_mx)
-                hold_clock()
             if i < CHUNKS:
                 grouped = [None] * TILES
                 for j in range(TILES):

@@ -24,7 +24,7 @@ HALVES = 2
 TILES = 4
 CHUNK_ROWS = TILES * P
 CHUNKS = T // CHUNK_ROWS
-VECTOR_TILE = TILES - 1
+VECTOR_EVERY = 3
 
 
 def tile_combcrossattention_pa_t_kernel(tc, hidden_states, Wq, q_norm_w, out):
@@ -139,7 +139,8 @@ def tile_combcrossattention_pa_t_kernel(tc, hidden_states, Wq, q_norm_w, out):
             if i < CHUNKS:
                 grouped = [None] * TILES
                 for j in range(TILES):
-                    copy = nc.vector.tensor_copy if j == VECTOR_TILE else nc.scalar.copy
+                    on_vector = (i * TILES + j) % VECTOR_EVERY == VECTOR_EVERY - 1
+                    copy = nc.vector.tensor_copy if on_vector else nc.scalar.copy
                     grouped[j] = regroup(copy, flipped[j])
                 x_mx = [quantise(grouped[j], mx_pool) for j in range(TILES)]
             if i > 0:

@@ -22,9 +22,9 @@ K_PASS = P * PACK
 PASSES = E // K_PASS
 HALVES = 2
 TILES = 4
-CHUNK_ROWS = TILES * P
-CHUNKS = T // CHUNK_ROWS
-VECTOR_EVERY = 3
+CHUNKS = T // (TILES * P)
+VECTOR_TILES = 2
+OF_TILES = 7
 
 
 def tile_combcrossattention_pa_t_kernel(tc, hidden_states, Wq, q_norm_w, out):
@@ -38,10 +38,12 @@ def tile_combcrossattention_pa_t_kernel(tc, hidden_states, Wq, q_norm_w, out):
         group_pool = ctx.enter_context(tc.tile_pool(name="group", bufs=2 * TILES))
         mx_pool = ctx.enter_context(tc.tile_pool(name="mx", bufs=2 * TILES))
         stat_pool = ctx.enter_context(tc.tile_pool(name="stat", bufs=3))
-        out_pool = ctx.enter_context(tc.tile_pool(name="outp", bufs=CHUNKS))
         flip_psum = ctx.enter_context(tc.psum_pool(name="flip", bufs=6))
         q_psum = ctx.enter_context(tc.psum_pool(name="q", bufs=2))
         ctx.enter_context(tc.manual_schedule())
+
+        def goes_to_vector(n):
+            return (n * VECTOR_TILES) % OF_TILES < VECTOR_TILES
 
         def transpose_rows(rows):
             words = rows.bitcast(F32)
@@ -84,7 +86,7 @@ def tile_combcrossattention_pa_t_kernel(tc, hidden_states, Wq, q_norm_w, out):
                     )
             return q
 
-        def inverse_rms(q):
+        def mean_squares(q):
             squares = stat_pool.tile([P, TILES, H, D], F32)
             mean_sq = stat_pool.tile([P, TILES, H], F32)
             for j in range(TILES):
@@ -96,12 +98,15 @@ def tile_combcrossattention_pa_t_kernel(tc, hidden_states, Wq, q_norm_w, out):
                         scale=1.0 / math.sqrt(D),
                         accum_out=mean_sq[:, j, h : h + 1],
                     )
+            return mean_sq
+
+        def inverse_root(mean_sq):
             rstd = stat_pool.tile([P, TILES, H], F32)
             nc.scalar.activation(out=rstd[:], in_=mean_sq[:], func=ACT.Abs_reciprocal_sqrt, bias=eps[:])
             return rstd
 
         def normalise_and_store(c, q, rstd):
-            normed = out_pool.tile([P, H, TILES, D], F32)
+            normed = resident.tile([P, H, TILES, D], F32, name="normed%d" % c)
             for j in range(TILES):
                 for h in range(H):
                     nc.vector.scalar_tensor_tensor(
@@ -118,31 +123,47 @@ def tile_combcrossattention_pa_t_kernel(tc, hidden_states, Wq, q_norm_w, out):
         make_identity(nc, ident[:])
         eps = const.tile([P, 1], F32)
         nc.vector.memset(eps[:], EPS)
+        first_use = const.tile([P, 1], F32)
+        nc.scalar.activation(out=first_use[:], in_=eps[:], func=ACT.Abs_reciprocal_sqrt)
         gain = const.tile([P, D], BF16)
         nc.scalar.dma_start(out=gain[:], in_=q_norm_w.partition_broadcast(P))
+
         w_rows = const.tile([P, E], BF16)
         nc.sync.dma_start(out=w_rows[:], in_=Wq)
         x_rows = []
         for c in range(CHUNKS):
             x_chunk = resident.tile([P, TILES, E], BF16, name="x%d" % c)
-            nc.sync.dma_start(out=x_chunk[:], in_=x_view[c])
+            if c == 0:
+                for j in range(TILES):
+                    nc.sync.dma_start(out=x_chunk[:, j, :], in_=x_view[c][:, j, :])
+            else:
+                nc.sync.dma_start(out=x_chunk[:], in_=x_view[c])
             x_rows.append(x_chunk)
 
         w_codes, w_scales = quantise(regroup(nc.vector.tensor_copy, transpose_rows(w_rows[:])), const)
+        flipped = [transpose_rows(x_rows[0][:, j, :]) for j in range(TILES)]
 
         x_mx = None
-        for i in range(CHUNKS + 1):
+        q = {}
+        mean_sq = {}
+        for i in range(CHUNKS + 2):
+            if 1 <= i <= CHUNKS:
+                q[i - 1] = project(x_mx)
             if i < CHUNKS:
-                flipped = [transpose_rows(x_rows[i][:, j, :]) for j in range(TILES)]
-            if i > 0:
-                q = project(x_mx)
+                vector_tiles = [j for j in range(TILES) if goes_to_vector(i * TILES + j)]
+                scalar_tiles = [j for j in range(TILES) if not goes_to_vector(i * TILES + j)]
+                grouped = {}
+                for j in vector_tiles:
+                    grouped[j] = regroup(nc.vector.tensor_copy, flipped[j])
+                for j in scalar_tiles:
+                    grouped[j] = regroup(nc.scalar.copy, flipped[j])
+            if i + 1 < CHUNKS:
+                flipped = [transpose_rows(x_rows[i + 1][:, j, :]) for j in range(TILES)]
             if i < CHUNKS:
-                grouped = [None] * TILES
-                for j in range(TILES):
-                    on_vector = (i * TILES + j) % VECTOR_EVERY == VECTOR_EVERY - 1
-                    copy = nc.vector.tensor_copy if on_vector else nc.scalar.copy
-                    grouped[j] = regroup(copy, flipped[j])
-                x_mx = [quantise(grouped[j], mx_pool) for j in range(TILES)]
-            if i > 0:
-                rstd = inverse_rms(q)
-                normalise_and_store(i - 1, q, rstd)
+                x_mx = {}
+                for j in scalar_tiles + vector_tiles:
+                    x_mx[j] = quantise(grouped[j], mx_pool)
+            if i >= 2:
+                normalise_and_store(i - 2, q[i - 2], inverse_root(mean_sq[i - 2]))
+            if 1 <= i <= CHUNKS:
+                mean_sq[i - 1] = mean_squares(q[i - 1])

@@ -21,29 +21,28 @@ PACK = 4
 K_PASS = P * PACK
 PASSES = E // K_PASS
 HALVES = 2
-TILES = 4
-CHUNKS = T // (TILES * P)
-VECTOR_TILES = 2
-OF_TILES = 7
+UNITS = (1, 1, 2) + 14 * (4,) + (2, 1, 1)
+VECTOR_TILES = (2, 61)
+STATS = 6
 
 
 def tile_combcrossattention_pa_t_kernel(tc, hidden_states, Wq, q_norm_w, out):
     nc = tc.nc
-    x_view = hidden_states.rearrange("(c p j) k -> c p j k", p=P, j=TILES)
-    out_view = out.rearrange("h (c p j) d -> c p h (j d)", p=P, j=TILES)
+    firsts = [sum(UNITS[:i]) for i in range(len(UNITS))]
+    count = len(UNITS)
 
     with ExitStack() as ctx:
         const = ctx.enter_context(tc.tile_pool(name="const", bufs=1))
         resident = ctx.enter_context(tc.tile_pool(name="resident", bufs=1))
-        group_pool = ctx.enter_context(tc.tile_pool(name="group", bufs=2 * TILES))
-        mx_pool = ctx.enter_context(tc.tile_pool(name="mx", bufs=2 * TILES))
+        group_pool = ctx.enter_context(tc.tile_pool(name="group", bufs=3))
+        mx_pool = ctx.enter_context(tc.tile_pool(name="mx", bufs=3))
         stat_pool = ctx.enter_context(tc.tile_pool(name="stat", bufs=3))
-        flip_psum = ctx.enter_context(tc.psum_pool(name="flip", bufs=6))
-        q_psum = ctx.enter_context(tc.psum_pool(name="q", bufs=2))
+        flip_psum = ctx.enter_context(tc.psum_pool(name="flip", bufs=5))
+        q_psum = ctx.enter_context(tc.psum_pool(name="q", bufs=3))
         ctx.enter_context(tc.manual_schedule())
 
         def goes_to_vector(n):
-            return (n * VECTOR_TILES) % OF_TILES < VECTOR_TILES
+            return n in VECTOR_TILES
 
         def transpose_rows(rows):
             words = rows.bitcast(F32)
@@ -54,60 +53,70 @@ def tile_combcrossattention_pa_t_kernel(tc, hidden_states, Wq, q_norm_w, out):
                     nc.tensor.transpose(flipped[:, g, u, :], words[:, first : first + P], ident[:])
             return flipped
 
-        def regroup(copy, flipped):
-            grouped = group_pool.tile([P, PASSES, P, PACK], BF16, align_bytes=64)
-            copy(out=grouped[:].bitcast(F32), in_=flipped[:].rearrange("p g u r -> p g r u"))
-            return grouped
+        def regroup(copy, flipped, grouped):
+            copy(out=grouped.bitcast(F32), in_=flipped[:].rearrange("p g u r -> p g r u"))
 
-        def quantise(grouped, pool):
-            codes = pool.tile([P, PASSES * P], U32, align_bytes=64)
-            scales = pool.tile([P, PASSES * P], U8, align_bytes=64)
+        def quantise(grouped, n, pool):
+            codes = pool.tile([P, n * PASSES * P], U32, align_bytes=64)
+            scales = pool.tile([P, n * PASSES * P], U8, align_bytes=64)
             nc.vector.quantize_mx(
                 out=codes[:].bitcast(FP8X4),
                 scales=scales[:],
-                in_=grouped[:].rearrange("p g r e -> p (g r e)"),
+                in_=grouped[:].rearrange("p j g r e -> p (j g r e)"),
             )
             return codes, scales
 
-        def project(x_mx):
-            q = q_psum.tile([P, TILES, H * D], F32)
-            for j in range(TILES):
-                codes, scales = x_mx[j]
+        def project(x_mx, n):
+            q = q_psum.tile([P, 4, H * D], F32)
+            codes, scales = x_mx
+            for j in range(n):
                 for g in range(PASSES):
-                    cols = slice(g * P, (g + 1) * P)
+                    cols = slice((j * PASSES + g) * P, (j * PASSES + g + 1) * P)
+                    w_cols = slice(g * P, (g + 1) * P)
                     nc.tensor.matmul_mx(
                         out=q[:, j, :],
                         lhsT=codes[:, cols].bitcast(FP8X4),
                         lhsT_scale=scales[:, cols],
-                        rhs=w_codes[:, cols].bitcast(FP8X4),
-                        rhs_scale=w_scales[:, cols],
+                        rhs=w_codes[:, w_cols].bitcast(FP8X4),
+                        rhs_scale=w_scales[:, w_cols],
                         start=(g == 0),
                         stop=(g == PASSES - 1),
                     )
             return q
 
-        def mean_squares(q):
-            squares = stat_pool.tile([P, TILES, H, D], F32)
-            mean_sq = stat_pool.tile([P, TILES, H], F32)
-            for j in range(TILES):
-                for h in range(H):
-                    nc.scalar.activation(
-                        out=squares[:, j, h, :],
-                        in_=q[:, j, h * D : (h + 1) * D],
-                        func=ACT.Square,
-                        scale=1.0 / math.sqrt(D),
-                        accum_out=mean_sq[:, j, h : h + 1],
-                    )
-            return mean_sq
+        def statistics(q, n):
+            stats = stat_pool.tile([P, 4, STATS], F32)
+            for j in range(n):
+                nc.vector.bn_stats(out=stats[:, j, :], in_=q[:, j, :].rearrange("p (h d) -> p d h", h=H))
+            return stats
 
-        def inverse_root(mean_sq):
-            rstd = stat_pool.tile([P, TILES, H], F32)
-            nc.scalar.activation(out=rstd[:], in_=mean_sq[:], func=ACT.Abs_reciprocal_sqrt, bias=eps[:])
+        def squared_sum_of_means(stats, n):
+            mean_part = stat_pool.tile([P, 4, H], F32)
+            nc.scalar.activation(
+                out=mean_part[:, :n, :], in_=stats[:, :n, 1::3], func=ACT.Square, scale=math.sqrt(D)
+            )
+            return mean_part
+
+        def sum_squares(stats, mean_part, n):
+            total = stat_pool.tile([P, 4, H], F32)
+            nc.vector.tensor_add(out=total[:, :n, :], in0=stats[:, :n, 2::3], in1=mean_part[:, :n, :])
+            return total
+
+        def inverse_root(total, n):
+            rstd = stat_pool.tile([P, 4, H], F32)
+            nc.scalar.activation(
+                out=rstd[:, :n, :],
+                in_=total[:, :n, :],
+                func=ACT.Abs_reciprocal_sqrt,
+                bias=eps[:],
+                scale=1.0 / D,
+            )
             return rstd
 
-        def normalise_and_store(c, q, rstd):
-            normed = resident.tile([P, H, TILES, D], F32, name="normed%d" % c)
-            for j in range(TILES):
+        def normalise_and_store(i, q, rstd):
+            n = UNITS[i]
+            normed = resident.tile([P, H, n, D], F32, name="normed%d" % i)
+            for j in range(n):
                 for h in range(H):
                     nc.vector.scalar_tensor_tensor(
                         out=normed[:, h, j, :],
@@ -117,7 +126,11 @@ def tile_combcrossattention_pa_t_kernel(tc, hidden_states, Wq, q_norm_w, out):
                         op0=ALU.mult,
                         op1=ALU.mult,
                     )
-            nc.sync.dma_start(out=out_view[c], in_=normed[:].rearrange("p h j d -> p h (j d)"))
+            rows = slice(firsts[i] * P, (firsts[i] + n) * P)
+            nc.sync.dma_start(
+                out=out[:, rows, :].rearrange("h (p j) d -> p h (j d)", j=n),
+                in_=normed[:].rearrange("p h j d -> p h (j d)"),
+            )
 
         ident = const.tile([P, P], F32)
         make_identity(nc, ident[:])
@@ -129,41 +142,58 @@ def tile_combcrossattention_pa_t_kernel(tc, hidden_states, Wq, q_norm_w, out):
         nc.scalar.dma_start(out=gain[:], in_=q_norm_w.partition_broadcast(P))
 
         w_rows = const.tile([P, E], BF16)
-        nc.sync.dma_start(out=w_rows[:], in_=Wq)
         x_rows = []
-        for c in range(CHUNKS):
-            x_chunk = resident.tile([P, TILES, E], BF16, name="x%d" % c)
-            if c == 0:
-                for j in range(TILES):
-                    nc.sync.dma_start(out=x_chunk[:, j, :], in_=x_view[c][:, j, :])
-            else:
-                nc.sync.dma_start(out=x_chunk[:], in_=x_view[c])
-            x_rows.append(x_chunk)
+        for i in range(count):
+            n = UNITS[i]
+            x_unit = resident.tile([P, n, E], BF16, name="x%d" % i)
+            rows = slice(firsts[i] * P, (firsts[i] + n) * P)
+            nc.sync.dma_start(
+                out=x_unit[:], in_=hidden_states[rows, :].rearrange("(p j) k -> p j k", j=n)
+            )
+            x_rows.append(x_unit)
+            if i == 0:
+                nc.sync.dma_start(out=w_rows[:], in_=Wq)
 
-        w_codes, w_scales = quantise(regroup(nc.vector.tensor_copy, transpose_rows(w_rows[:])), const)
-        flipped = [transpose_rows(x_rows[0][:, j, :]) for j in range(TILES)]
-
-        x_mx = None
+        flipped = {}
+        grouped = {}
+        x_mx = {}
         q = {}
-        mean_sq = {}
-        for i in range(CHUNKS + 2):
-            if 1 <= i <= CHUNKS:
-                q[i - 1] = project(x_mx)
-            if i < CHUNKS:
-                vector_tiles = [j for j in range(TILES) if goes_to_vector(i * TILES + j)]
-                scalar_tiles = [j for j in range(TILES) if not goes_to_vector(i * TILES + j)]
-                grouped = {}
+        flipped[0] = [transpose_rows(x_rows[0][:, 0, :])]
+        w_flipped = transpose_rows(w_rows[:])
+        w_grouped = const.tile([P, 1, PASSES, P, PACK], BF16, align_bytes=64)
+
+        stats = {}
+        mean_part = {}
+        for i in range(count + 3):
+            this, done = i < count, 0 <= i - 3 < count
+            if 0 <= i - 2 < count:
+                q[i - 2] = project(x_mx[i - 2], UNITS[i - 2])
+            if done:
+                total = sum_squares(stats[i - 3], mean_part[i - 3], UNITS[i - 3])
+            if this:
+                unit_grouped = group_pool.tile([P, UNITS[i], PASSES, P, PACK], BF16, align_bytes=64)
+                grouped[i] = unit_grouped
+                vector_tiles = [j for j in range(UNITS[i]) if goes_to_vector(firsts[i] + j)]
+                scalar_tiles = [j for j in range(UNITS[i]) if not goes_to_vector(firsts[i] + j)]
                 for j in vector_tiles:
-                    grouped[j] = regroup(nc.vector.tensor_copy, flipped[j])
-                for j in scalar_tiles:
-                    grouped[j] = regroup(nc.scalar.copy, flipped[j])
-            if i + 1 < CHUNKS:
-                flipped = [transpose_rows(x_rows[i + 1][:, j, :]) for j in range(TILES)]
-            if i < CHUNKS:
-                x_mx = {}
-                for j in scalar_tiles + vector_tiles:
-                    x_mx[j] = quantise(grouped[j], mx_pool)
-            if i >= 2:
-                normalise_and_store(i - 2, q[i - 2], inverse_root(mean_sq[i - 2]))
-            if 1 <= i <= CHUNKS:
-                mean_sq[i - 1] = mean_squares(q[i - 1])
+                    regroup(nc.vector.tensor_copy, flipped[i][j], unit_grouped[:, j])
+                for j in scalar_tiles[:1]:
+                    regroup(nc.scalar.copy, flipped[i][j], unit_grouped[:, j])
+            if done:
+                rstd = inverse_root(total, UNITS[i - 3])
+            if this:
+                for j in scalar_tiles[1:]:
+                    regroup(nc.scalar.copy, flipped[i][j], unit_grouped[:, j])
+            if i == 0:
+                regroup(nc.vector.tensor_copy, w_flipped, w_grouped[:, 0])
+            if i + 1 < count:
+                flipped[i + 1] = [transpose_rows(x_rows[i + 1][:, j, :]) for j in range(UNITS[i + 1])]
+            if 0 <= i - 1 < count:
+                if i == 1:
+                    w_codes, w_scales = quantise(w_grouped, 1, const)
+                x_mx[i - 1] = quantise(grouped[i - 1], UNITS[i - 1], mx_pool)
+            if 0 <= i - 2 < count:
+                stats[i - 2] = statistics(q[i - 2], UNITS[i - 2])
+                mean_part[i - 2] = squared_sum_of_means(stats[i - 2], UNITS[i - 2])
+            if done:
+                normalise_and_store(i - 3, q[i - 3], rstd)

@@ -21,8 +21,9 @@ PACK = 4
 K_PASS = P * PACK
 PASSES = E // K_PASS
 HALVES = 2
-UNITS = (1, 1, 2) + 14 * (4,) + (2, 1, 1)
-VECTOR_TILES = (2, 61)
+UNITS = (1, 1, 2) + 19 * (3,) + (2, 1)
+VECTOR_TILES = (2, 4)
+S_FIRST = 2
 STATS = 6
 
 
@@ -44,6 +45,9 @@ def tile_combcrossattention_pa_t_kernel(tc, hidden_states, Wq, q_norm_w, out):
         def goes_to_vector(n):
             return n in VECTOR_TILES
 
+        def scalar_squares(i):
+            return UNITS[i] if i > count - 5 or i % 4 == 2 else 0
+
         def transpose_rows(rows):
             words = rows.bitcast(F32)
             flipped = flip_psum.tile([P, PASSES, HALVES, P], F32)
@@ -59,11 +63,14 @@ def tile_combcrossattention_pa_t_kernel(tc, hidden_states, Wq, q_norm_w, out):
         def quantise(grouped, n, pool):
             codes = pool.tile([P, n * PASSES * P], U32, align_bytes=64)
             scales = pool.tile([P, n * PASSES * P], U8, align_bytes=64)
-            nc.vector.quantize_mx(
-                out=codes[:].bitcast(FP8X4),
-                scales=scales[:],
-                in_=grouped[:].rearrange("p j g r e -> p (j g r e)"),
-            )
+            for first in range(0, n, 2):
+                tiles = slice(first, min(first + 2, n))
+                words = slice(first * PASSES * P, min(first + 2, n) * PASSES * P)
+                nc.vector.quantize_mx(
+                    out=codes[:, words].bitcast(FP8X4),
+                    scales=scales[:, words],
+                    in_=grouped[:, tiles].rearrange("p j g r e -> p (j g r e)"),
+                )
             return codes, scales
 
         def project(x_mx, n):
@@ -84,23 +91,39 @@ def tile_combcrossattention_pa_t_kernel(tc, hidden_states, Wq, q_norm_w, out):
                     )
             return q
 
-        def statistics(q, n):
+        def statistics(q, n, m):
             stats = stat_pool.tile([P, 4, STATS], F32)
-            for j in range(n):
+            for j in range(m, n):
                 nc.vector.bn_stats(out=stats[:, j, :], in_=q[:, j, :].rearrange("p (h d) -> p d h", h=H))
             return stats
 
-        def squared_sum_of_means(stats, n):
+        def scalar_sums(q, m):
+            total = stat_pool.tile([P, 4, H], F32)
+            squares = stat_pool.tile([P, 4, H, D], F32)
+            for j in range(m):
+                for h in range(H):
+                    nc.scalar.activation(
+                        out=squares[:, j, h, :],
+                        in_=q[:, j, h * D : (h + 1) * D],
+                        func=ACT.Square,
+                        accum_out=total[:, j, h : h + 1],
+                    )
+            return total
+
+        def means_part(stats, n, m):
             mean_part = stat_pool.tile([P, 4, H], F32)
-            nc.scalar.activation(
-                out=mean_part[:, :n, :], in_=stats[:, :n, 1::3], func=ACT.Square, scale=math.sqrt(D)
+            nc.vector.scalar_tensor_tensor(
+                out=mean_part[:, m:n, :],
+                in0=stats[:, m:n, 1::3],
+                scalar=float(D),
+                in1=stats[:, m:n, 1::3],
+                op0=ALU.mult,
+                op1=ALU.mult,
             )
             return mean_part
 
-        def sum_squares(stats, mean_part, n):
-            total = stat_pool.tile([P, 4, H], F32)
-            nc.vector.tensor_add(out=total[:, :n, :], in0=stats[:, :n, 2::3], in1=mean_part[:, :n, :])
-            return total
+        def vector_sums(stats, mean_part, total, n, m):
+            nc.vector.tensor_add(out=total[:, m:n, :], in0=stats[:, m:n, 2::3], in1=mean_part[:, m:n, :])
 
         def inverse_root(total, n):
             rstd = stat_pool.tile([P, 4, H], F32)
@@ -113,19 +136,19 @@ def tile_combcrossattention_pa_t_kernel(tc, hidden_states, Wq, q_norm_w, out):
             )
             return rstd
 
-        def normalise_and_store(i, q, rstd):
+        def normalise(i, q, rstd, normed, h):
+            for j in range(UNITS[i]):
+                nc.vector.scalar_tensor_tensor(
+                    out=normed[:, h, j, :],
+                    in0=q[:, j, h * D : (h + 1) * D],
+                    scalar=rstd[:, j, h : h + 1],
+                    in1=gain[:],
+                    op0=ALU.mult,
+                    op1=ALU.mult,
+                )
+
+        def store(i, normed):
             n = UNITS[i]
-            normed = resident.tile([P, H, n, D], F32, name="normed%d" % i)
-            for j in range(n):
-                for h in range(H):
-                    nc.vector.scalar_tensor_tensor(
-                        out=normed[:, h, j, :],
-                        in0=q[:, j, h * D : (h + 1) * D],
-                        scalar=rstd[:, j, h : h + 1],
-                        in1=gain[:],
-                        op0=ALU.mult,
-                        op1=ALU.mult,
-                    )
             rows = slice(firsts[i] * P, (firsts[i] + n) * P)
             nc.sync.dma_start(
                 out=out[:, rows, :].rearrange("h (p j) d -> p h (j d)", j=n),
@@ -162,14 +185,11 @@ def tile_combcrossattention_pa_t_kernel(tc, hidden_states, Wq, q_norm_w, out):
         w_flipped = transpose_rows(w_rows[:])
         w_grouped = const.tile([P, 1, PASSES, P, PACK], BF16, align_bytes=64)
 
-        stats = {}
-        mean_part = {}
+        total = {}
         for i in range(count + 3):
             this, done = i < count, 0 <= i - 3 < count
             if 0 <= i - 2 < count:
                 q[i - 2] = project(x_mx[i - 2], UNITS[i - 2])
-            if done:
-                total = sum_squares(stats[i - 3], mean_part[i - 3], UNITS[i - 3])
             if this:
                 unit_grouped = group_pool.tile([P, UNITS[i], PASSES, P, PACK], BF16, align_bytes=64)
                 grouped[i] = unit_grouped
@@ -177,12 +197,12 @@ def tile_combcrossattention_pa_t_kernel(tc, hidden_states, Wq, q_norm_w, out):
                 scalar_tiles = [j for j in range(UNITS[i]) if not goes_to_vector(firsts[i] + j)]
                 for j in vector_tiles:
                     regroup(nc.vector.tensor_copy, flipped[i][j], unit_grouped[:, j])
-                for j in scalar_tiles[:1]:
+                for j in scalar_tiles[:S_FIRST]:
                     regroup(nc.scalar.copy, flipped[i][j], unit_grouped[:, j])
             if done:
-                rstd = inverse_root(total, UNITS[i - 3])
+                rstd = inverse_root(total[i - 3], UNITS[i - 3])
             if this:
-                for j in scalar_tiles[1:]:
+                for j in scalar_tiles[S_FIRST:]:
                     regroup(nc.scalar.copy, flipped[i][j], unit_grouped[:, j])
             if i == 0:
                 regroup(nc.vector.tensor_copy, w_flipped, w_grouped[:, 0])
@@ -192,8 +212,18 @@ def tile_combcrossattention_pa_t_kernel(tc, hidden_states, Wq, q_norm_w, out):
                 if i == 1:
                     w_codes, w_scales = quantise(w_grouped, 1, const)
                 x_mx[i - 1] = quantise(grouped[i - 1], UNITS[i - 1], mx_pool)
-            if 0 <= i - 2 < count:
-                stats[i - 2] = statistics(q[i - 2], UNITS[i - 2])
-                mean_part[i - 2] = squared_sum_of_means(stats[i - 2], UNITS[i - 2])
+            fresh = 0 <= i - 2 < count
+            if fresh:
+                n, m = UNITS[i - 2], scalar_squares(i - 2)
+                stats = statistics(q[i - 2], n, m)
+                total[i - 2] = scalar_sums(q[i - 2], m)
             if done:
-                normalise_and_store(i - 3, q[i - 3], rstd)
+                normed = resident.tile([P, H, UNITS[i - 3], D], F32, name="normed%d" % (i - 3))
+                normalise(i - 3, q[i - 3], rstd, normed, 0)
+            if fresh and m < n:
+                mean_part = means_part(stats, n, m)
+            if done:
+                normalise(i - 3, q[i - 3], rstd, normed, 1)
+                store(i - 3, normed)
+            if fresh and m < n:
+                vector_sums(stats, mean_part, total[i - 2], n, m)

@@ -21,7 +21,8 @@ PACK = 4
 K_PASS = P * PACK
 PASSES = E // K_PASS
 HALVES = 2
-UNITS = (1, 1, 2) + 19 * (3,) + (2, 1)
+GROUPS = ((1, 1, 2),) + 4 * ((3, 3, 3, 3),) + ((3, 3), (3,), (2,), (1,))
+UNITS = tuple(n for group in GROUPS for n in group)
 VECTOR_TILES = (2, 4)
 S_FIRST = 2
 STATS = 6
@@ -31,6 +32,9 @@ def tile_combcrossattention_pa_t_kernel(tc, hidden_states, Wq, q_norm_w, out):
     nc = tc.nc
     firsts = [sum(UNITS[:i]) for i in range(len(UNITS))]
     count = len(UNITS)
+    group_of = [g for g, group in enumerate(GROUPS) for n in group]
+    group_sizes = [sum(group) for group in GROUPS]
+    group_firsts = [sum(group_sizes[:g]) for g in range(len(GROUPS))]
 
     with ExitStack() as ctx:
         const = ctx.enter_context(tc.tile_pool(name="const", bufs=1))
@@ -136,10 +140,11 @@ def tile_combcrossattention_pa_t_kernel(tc, hidden_states, Wq, q_norm_w, out):
             )
             return rstd
 
-        def normalise(i, q, rstd, normed, h):
+        def normalise(i, q, rstd, h):
+            g = group_of[i]
             for j in range(UNITS[i]):
                 nc.vector.scalar_tensor_tensor(
-                    out=normed[:, h, j, :],
+                    out=normed[g][:, h, firsts[i] - group_firsts[g] + j, :],
                     in0=q[:, j, h * D : (h + 1) * D],
                     scalar=rstd[:, j, h : h + 1],
                     in1=gain[:],
@@ -147,12 +152,11 @@ def tile_combcrossattention_pa_t_kernel(tc, hidden_states, Wq, q_norm_w, out):
                     op1=ALU.mult,
                 )
 
-        def store(i, normed):
-            n = UNITS[i]
-            rows = slice(firsts[i] * P, (firsts[i] + n) * P)
+        def store(g):
+            rows = slice(group_firsts[g] * P, (group_firsts[g] + group_sizes[g]) * P)
             nc.sync.dma_start(
-                out=out[:, rows, :].rearrange("h (p j) d -> p h (j d)", j=n),
-                in_=normed[:].rearrange("p h j d -> p h (j d)"),
+                out=out[:, rows, :].rearrange("h (p j) d -> p h (j d)", j=group_sizes[g]),
+                in_=normed[g][:].rearrange("p h j d -> p h (j d)"),
             )
 
         ident = const.tile([P, P], F32)
@@ -169,10 +173,11 @@ def tile_combcrossattention_pa_t_kernel(tc, hidden_states, Wq, q_norm_w, out):
         for i in range(count):
             n = UNITS[i]
             x_unit = resident.tile([P, n, E], BF16, name="x%d" % i)
-            rows = slice(firsts[i] * P, (firsts[i] + n) * P)
-            nc.sync.dma_start(
-                out=x_unit[:], in_=hidden_states[rows, :].rearrange("(p j) k -> p j k", j=n)
-            )
+            g = group_of[i]
+            rows = slice(group_firsts[g] * P, (group_firsts[g] + group_sizes[g]) * P)
+            x_group = hidden_states[rows, :].rearrange("(p j) k -> p j k", j=group_sizes[g])
+            j = firsts[i] - group_firsts[g]
+            nc.sync.dma_start(out=x_unit[:], in_=x_group[:, j : j + n])
             x_rows.append(x_unit)
             if i == 0:
                 nc.sync.dma_start(out=w_rows[:], in_=Wq)
@@ -186,6 +191,10 @@ def tile_combcrossattention_pa_t_kernel(tc, hidden_states, Wq, q_norm_w, out):
         w_grouped = const.tile([P, 1, PASSES, P, PACK], BF16, align_bytes=64)
 
         total = {}
+        normed = []
+        for g in range(len(GROUPS)):
+            normed_group = resident.tile([P, H, group_sizes[g], D], F32, name="normed%d" % g)
+            normed.append(normed_group)
         for i in range(count + 3):
             this, done = i < count, 0 <= i - 3 < count
             if 0 <= i - 2 < count:
@@ -218,12 +227,12 @@ def tile_combcrossattention_pa_t_kernel(tc, hidden_states, Wq, q_norm_w, out):
                 stats = statistics(q[i - 2], n, m)
                 total[i - 2] = scalar_sums(q[i - 2], m)
             if done:
-                normed = resident.tile([P, H, UNITS[i - 3], D], F32, name="normed%d" % (i - 3))
-                normalise(i - 3, q[i - 3], rstd, normed, 0)
+                normalise(i - 3, q[i - 3], rstd, 0)
             if fresh and m < n:
                 mean_part = means_part(stats, n, m)
             if done:
-                normalise(i - 3, q[i - 3], rstd, normed, 1)
-                store(i - 3, normed)
+                normalise(i - 3, q[i - 3], rstd, 1)
+                if i - 3 == count - 1 or group_of[i - 2] != group_of[i - 3]:
+                    store(group_of[i - 3])
             if fresh and m < n:
                 vector_sums(stats, mean_part, total[i - 2], n, m)

@@ -21,9 +21,9 @@ PACK = 4
 K_PASS = P * PACK
 PASSES = E // K_PASS
 HALVES = 2
-GROUPS = ((1, 1, 2),) + 4 * ((3, 3, 3, 3),) + ((3, 3), (3,), (2,), (1,))
+GROUPS = ((1, 3),) + 4 * ((3, 3, 3, 3),) + ((3, 3), (3,), (2,), (1,))
 UNITS = tuple(n for group in GROUPS for n in group)
-VECTOR_TILES = (2, 4)
+VECTOR_TILES = ()
 S_FIRST = 2
 STATS = 6
 
@@ -50,7 +50,7 @@ def tile_combcrossattention_pa_t_kernel(tc, hidden_states, Wq, q_norm_w, out):
             return n in VECTOR_TILES
 
         def scalar_squares(i):
-            return UNITS[i] if i > count - 5 or i % 4 == 2 else 0
+            return UNITS[i] if i > count - 5 else i % 2
 
         def transpose_rows(rows):
             words = rows.bitcast(F32)
@@ -64,18 +64,13 @@ def tile_combcrossattention_pa_t_kernel(tc, hidden_states, Wq, q_norm_w, out):
         def regroup(copy, flipped, grouped):
             copy(out=grouped.bitcast(F32), in_=flipped[:].rearrange("p g u r -> p g r u"))
 
-        def quantise(grouped, n, pool):
-            codes = pool.tile([P, n * PASSES * P], U32, align_bytes=64)
-            scales = pool.tile([P, n * PASSES * P], U8, align_bytes=64)
-            for first in range(0, n, 2):
-                tiles = slice(first, min(first + 2, n))
-                words = slice(first * PASSES * P, min(first + 2, n) * PASSES * P)
-                nc.vector.quantize_mx(
-                    out=codes[:, words].bitcast(FP8X4),
-                    scales=scales[:, words],
-                    in_=grouped[:, tiles].rearrange("p j g r e -> p (j g r e)"),
-                )
-            return codes, scales
+        def quantise(grouped, codes, scales, first, last):
+            words = slice(first * PASSES * P, last * PASSES * P)
+            nc.vector.quantize_mx(
+                out=codes[:, words].bitcast(FP8X4),
+                scales=scales[:, words],
+                in_=grouped[:, first:last].rearrange("p j g r e -> p (j g r e)"),
+            )
 
         def project(x_mx, n):
             q = q_psum.tile([P, 4, H * D], F32)
@@ -114,15 +109,10 @@ def tile_combcrossattention_pa_t_kernel(tc, hidden_states, Wq, q_norm_w, out):
                     )
             return total
 
-        def means_part(stats, n, m):
+        def squared_means(stats, n, m):
             mean_part = stat_pool.tile([P, 4, H], F32)
-            nc.vector.scalar_tensor_tensor(
-                out=mean_part[:, m:n, :],
-                in0=stats[:, m:n, 1::3],
-                scalar=float(D),
-                in1=stats[:, m:n, 1::3],
-                op0=ALU.mult,
-                op1=ALU.mult,
+            nc.scalar.activation(
+                out=mean_part[:, m:n, :], in_=stats[:, m:n, 1::3], func=ACT.Square, scale=math.sqrt(D)
             )
             return mean_part
 
@@ -140,9 +130,10 @@ def tile_combcrossattention_pa_t_kernel(tc, hidden_states, Wq, q_norm_w, out):
             )
             return rstd
 
-        def normalise(i, q, rstd, h):
+        def normalise(i, q, rstd, first, last):
             g = group_of[i]
-            for j in range(UNITS[i]):
+            pairs = [(h, j) for h in range(H) for j in range(UNITS[i])]
+            for h, j in pairs[first:last]:
                 nc.vector.scalar_tensor_tensor(
                     out=normed[g][:, h, firsts[i] - group_firsts[g] + j, :],
                     in0=q[:, j, h * D : (h + 1) * D],
@@ -188,16 +179,20 @@ def tile_combcrossattention_pa_t_kernel(tc, hidden_states, Wq, q_norm_w, out):
         q = {}
         flipped[0] = [transpose_rows(x_rows[0][:, 0, :])]
         w_flipped = transpose_rows(w_rows[:])
+        w_codes = const.tile([P, PASSES * P], U32, align_bytes=64)
+        w_scales = const.tile([P, PASSES * P], U8, align_bytes=64)
         w_grouped = const.tile([P, 1, PASSES, P, PACK], BF16, align_bytes=64)
 
         total = {}
+        stats = {}
+        mean_part = {}
         normed = []
         for g in range(len(GROUPS)):
             normed_group = resident.tile([P, H, group_sizes[g], D], F32, name="normed%d" % g)
             normed.append(normed_group)
         for i in range(count + 3):
-            this, done = i < count, 0 <= i - 3 < count
-            if 0 <= i - 2 < count:
+            this, done, fresh = i < count, 0 <= i - 3 < count, 0 <= i - 2 < count
+            if fresh:
                 q[i - 2] = project(x_mx[i - 2], UNITS[i - 2])
             if this:
                 unit_grouped = group_pool.tile([P, UNITS[i], PASSES, P, PACK], BF16, align_bytes=64)
@@ -208,31 +203,34 @@ def tile_combcrossattention_pa_t_kernel(tc, hidden_states, Wq, q_norm_w, out):
                     regroup(nc.vector.tensor_copy, flipped[i][j], unit_grouped[:, j])
                 for j in scalar_tiles[:S_FIRST]:
                     regroup(nc.scalar.copy, flipped[i][j], unit_grouped[:, j])
+            if i == 0:
+                regroup(nc.vector.tensor_copy, w_flipped, w_grouped[:, 0])
+            if i == 1:
+                quantise(w_grouped, w_codes, w_scales, 0, 1)
+            n = UNITS[i - 1] if 0 <= i - 1 < count else 0
+            if n:
+                codes = mx_pool.tile([P, n * PASSES * P], U32, align_bytes=64)
+                scales = mx_pool.tile([P, n * PASSES * P], U8, align_bytes=64)
+                x_mx[i - 1] = codes, scales
+                quantise(grouped[i - 1], codes, scales, 0, min(n, 2))
+            if done and scalar_squares(i - 3) < UNITS[i - 3]:
+                vector_sums(stats[i - 3], mean_part[i - 3], total[i - 3], UNITS[i - 3], scalar_squares(i - 3))
+            if n > 2:
+                quantise(grouped[i - 1], codes, scales, 2, n)
+            if fresh:
+                stats[i - 2] = statistics(q[i - 2], UNITS[i - 2], scalar_squares(i - 2))
             if done:
                 rstd = inverse_root(total[i - 3], UNITS[i - 3])
             if this:
                 for j in scalar_tiles[S_FIRST:]:
                     regroup(nc.scalar.copy, flipped[i][j], unit_grouped[:, j])
-            if i == 0:
-                regroup(nc.vector.tensor_copy, w_flipped, w_grouped[:, 0])
             if i + 1 < count:
                 flipped[i + 1] = [transpose_rows(x_rows[i + 1][:, j, :]) for j in range(UNITS[i + 1])]
-            if 0 <= i - 1 < count:
-                if i == 1:
-                    w_codes, w_scales = quantise(w_grouped, 1, const)
-                x_mx[i - 1] = quantise(grouped[i - 1], UNITS[i - 1], mx_pool)
-            fresh = 0 <= i - 2 < count
             if fresh:
-                n, m = UNITS[i - 2], scalar_squares(i - 2)
-                stats = statistics(q[i - 2], n, m)
-                total[i - 2] = scalar_sums(q[i - 2], m)
+                total[i - 2] = scalar_sums(q[i - 2], scalar_squares(i - 2))
+                if scalar_squares(i - 2) < UNITS[i - 2]:
+                    mean_part[i - 2] = squared_means(stats[i - 2], UNITS[i - 2], scalar_squares(i - 2))
             if done:
-                normalise(i - 3, q[i - 3], rstd, 0)
-            if fresh and m < n:
-                mean_part = means_part(stats, n, m)
-            if done:
-                normalise(i - 3, q[i - 3], rstd, 1)
+                normalise(i - 3, q[i - 3], rstd, 0, H * UNITS[i - 3])
                 if i - 3 == count - 1 or group_of[i - 2] != group_of[i - 3]:
                     store(group_of[i - 3])
-            if fresh and m < n:
-                vector_sums(stats, mean_part, total[i - 2], n, m)

@@ -23,7 +23,7 @@ PASSES = E // K_PASS
 HALVES = 2
 GROUPS = ((1, 3),) + 4 * ((3, 3, 3, 3),) + ((3, 3), (3,), (2,), (1,))
 UNITS = tuple(n for group in GROUPS for n in group)
-VECTOR_TILES = ()
+BATCHES = (1, 1, 1) + 8 * (2,) + 4 * (1,)
 S_FIRST = 2
 STATS = 6
 
@@ -36,21 +36,27 @@ def tile_combcrossattention_pa_t_kernel(tc, hidden_states, Wq, q_norm_w, out):
     group_sizes = [sum(group) for group in GROUPS]
     group_firsts = [sum(group_sizes[:g]) for g in range(len(GROUPS))]
 
+    batch_of = [b for b, n in enumerate(BATCHES) for u in range(n)]
+    batch_firsts = [sum(BATCHES[:b]) for b in range(len(BATCHES))]
+    tiles_in = [sum(UNITS[f : f + n]) for f, n in zip(batch_firsts, BATCHES)]
+    offset = [firsts[i] - firsts[batch_firsts[batch_of[i]]] for i in range(count)]
+    scaling_round = [batch_firsts[b] + BATCHES[b] - 1 + 3 + u for b in range(len(BATCHES)) for u in range(BATCHES[b])]
+    most = max(tiles_in)
+
     with ExitStack() as ctx:
         const = ctx.enter_context(tc.tile_pool(name="const", bufs=1))
         resident = ctx.enter_context(tc.tile_pool(name="resident", bufs=1))
         group_pool = ctx.enter_context(tc.tile_pool(name="group", bufs=3))
         mx_pool = ctx.enter_context(tc.tile_pool(name="mx", bufs=3))
         stat_pool = ctx.enter_context(tc.tile_pool(name="stat", bufs=3))
-        flip_psum = ctx.enter_context(tc.psum_pool(name="flip", bufs=5))
-        q_psum = ctx.enter_context(tc.psum_pool(name="q", bufs=3))
+        flip_psum = ctx.enter_context(tc.psum_pool(name="flip", bufs=4))
+        q_psum = ctx.enter_context(tc.psum_pool(name="q", bufs=4))
         ctx.enter_context(tc.manual_schedule())
 
-        def goes_to_vector(n):
-            return n in VECTOR_TILES
-
-        def scalar_squares(i):
-            return UNITS[i] if i > count - 5 else i % 2
+        def scalar_squares(b):
+            if b >= len(BATCHES) - 4:
+                return tiles_in[b]
+            return 1 if BATCHES[b] == 2 else 0
 
         def transpose_rows(rows):
             words = rows.bitcast(F32)
@@ -90,37 +96,40 @@ def tile_combcrossattention_pa_t_kernel(tc, hidden_states, Wq, q_norm_w, out):
                     )
             return q
 
-        def statistics(q, n, m):
-            stats = stat_pool.tile([P, 4, STATS], F32)
-            for j in range(m, n):
-                nc.vector.bn_stats(out=stats[:, j, :], in_=q[:, j, :].rearrange("p (h d) -> p d h", h=H))
-            return stats
+        def statistics(i, q, stats):
+            b = batch_of[i]
+            for j in range(UNITS[i]):
+                if offset[i] + j >= scalar_squares(b):
+                    nc.vector.bn_stats(out=stats[:, offset[i] + j, :], in_=q[:, j, :].rearrange("p (h d) -> p d h", h=H))
 
-        def scalar_sums(q, m):
-            total = stat_pool.tile([P, 4, H], F32)
+        def scalar_sums(i, q, total):
+            b = batch_of[i]
             squares = stat_pool.tile([P, 4, H, D], F32)
-            for j in range(m):
-                for h in range(H):
-                    nc.scalar.activation(
-                        out=squares[:, j, h, :],
-                        in_=q[:, j, h * D : (h + 1) * D],
-                        func=ACT.Square,
-                        accum_out=total[:, j, h : h + 1],
-                    )
-            return total
+            for j in range(UNITS[i]):
+                if offset[i] + j < scalar_squares(b):
+                    for h in range(H):
+                        nc.scalar.activation(
+                            out=squares[:, j, h, :],
+                            in_=q[:, j, h * D : (h + 1) * D],
+                            func=ACT.Square,
+                            accum_out=total[:, offset[i] + j, h : h + 1],
+                        )
 
-        def squared_means(stats, n, m):
-            mean_part = stat_pool.tile([P, 4, H], F32)
+        def squared_means(stats, b):
+            m, n = scalar_squares(b), tiles_in[b]
+            mean_part = stat_pool.tile([P, most, H], F32)
             nc.scalar.activation(
                 out=mean_part[:, m:n, :], in_=stats[:, m:n, 1::3], func=ACT.Square, scale=math.sqrt(D)
             )
             return mean_part
 
-        def vector_sums(stats, mean_part, total, n, m):
+        def vector_sums(stats, mean_part, total, b):
+            m, n = scalar_squares(b), tiles_in[b]
             nc.vector.tensor_add(out=total[:, m:n, :], in0=stats[:, m:n, 2::3], in1=mean_part[:, m:n, :])
 
-        def inverse_root(total, n):
-            rstd = stat_pool.tile([P, 4, H], F32)
+        def inverse_root(total, b):
+            n = tiles_in[b]
+            rstd = stat_pool.tile([P, most, H], F32)
             nc.scalar.activation(
                 out=rstd[:, :n, :],
                 in_=total[:, :n, :],
@@ -130,18 +139,18 @@ def tile_combcrossattention_pa_t_kernel(tc, hidden_states, Wq, q_norm_w, out):
             )
             return rstd
 
-        def normalise(i, q, rstd, first, last):
+        def normalise(i, q, rstd):
             g = group_of[i]
-            pairs = [(h, j) for h in range(H) for j in range(UNITS[i])]
-            for h, j in pairs[first:last]:
-                nc.vector.scalar_tensor_tensor(
-                    out=normed[g][:, h, firsts[i] - group_firsts[g] + j, :],
-                    in0=q[:, j, h * D : (h + 1) * D],
-                    scalar=rstd[:, j, h : h + 1],
-                    in1=gain[:],
-                    op0=ALU.mult,
-                    op1=ALU.mult,
-                )
+            for h in range(H):
+                for j in range(UNITS[i]):
+                    nc.vector.scalar_tensor_tensor(
+                        out=normed[g][:, h, firsts[i] - group_firsts[g] + j, :],
+                        in0=q[:, j, h * D : (h + 1) * D],
+                        scalar=rstd[:, offset[i] + j, h : h + 1],
+                        in1=gain[:],
+                        op0=ALU.mult,
+                        op1=ALU.mult,
+                    )
 
         def store(g):
             rows = slice(group_firsts[g] * P, (group_firsts[g] + group_sizes[g]) * P)
@@ -186,22 +195,21 @@ def tile_combcrossattention_pa_t_kernel(tc, hidden_states, Wq, q_norm_w, out):
         total = {}
         stats = {}
         mean_part = {}
+        rstd = {}
         normed = []
         for g in range(len(GROUPS)):
             normed_group = resident.tile([P, H, group_sizes[g], D], F32, name="normed%d" % g)
             normed.append(normed_group)
         for i in range(count + 3):
-            this, done, fresh = i < count, 0 <= i - 3 < count, 0 <= i - 2 < count
+            this, fresh = i < count, 0 <= i - 2 < count
+            closing = [b for b in range(len(BATCHES)) if batch_firsts[b] + BATCHES[b] - 1 == i - 3]
+            scaled = [u for u in range(count) if scaling_round[u] == i]
             if fresh:
                 q[i - 2] = project(x_mx[i - 2], UNITS[i - 2])
             if this:
                 unit_grouped = group_pool.tile([P, UNITS[i], PASSES, P, PACK], BF16, align_bytes=64)
                 grouped[i] = unit_grouped
-                vector_tiles = [j for j in range(UNITS[i]) if goes_to_vector(firsts[i] + j)]
-                scalar_tiles = [j for j in range(UNITS[i]) if not goes_to_vector(firsts[i] + j)]
-                for j in vector_tiles:
-                    regroup(nc.vector.tensor_copy, flipped[i][j], unit_grouped[:, j])
-                for j in scalar_tiles[:S_FIRST]:
+                for j in range(UNITS[i])[:S_FIRST]:
                     regroup(nc.scalar.copy, flipped[i][j], unit_grouped[:, j])
             if i == 0:
                 regroup(nc.vector.tensor_copy, w_flipped, w_grouped[:, 0])
@@ -213,24 +221,32 @@ def tile_combcrossattention_pa_t_kernel(tc, hidden_states, Wq, q_norm_w, out):
                 scales = mx_pool.tile([P, n * PASSES * P], U8, align_bytes=64)
                 x_mx[i - 1] = codes, scales
                 quantise(grouped[i - 1], codes, scales, 0, min(n, 2))
-            if done and scalar_squares(i - 3) < UNITS[i - 3]:
-                vector_sums(stats[i - 3], mean_part[i - 3], total[i - 3], UNITS[i - 3], scalar_squares(i - 3))
+            for b in closing:
+                if scalar_squares(b) < tiles_in[b]:
+                    vector_sums(stats[b], mean_part[b], total[b], b)
             if n > 2:
                 quantise(grouped[i - 1], codes, scales, 2, n)
             if fresh:
-                stats[i - 2] = statistics(q[i - 2], UNITS[i - 2], scalar_squares(i - 2))
-            if done:
-                rstd = inverse_root(total[i - 3], UNITS[i - 3])
+                b = batch_of[i - 2]
+                if i - 2 == batch_firsts[b]:
+                    batch_stats = stat_pool.tile([P, most, STATS], F32)
+                    stats[b] = batch_stats
+                    batch_total = stat_pool.tile([P, most, H], F32)
+                    total[b] = batch_total
+                statistics(i - 2, q[i - 2], stats[b])
+            for b in closing:
+                rstd[b] = inverse_root(total[b], b)
             if this:
-                for j in scalar_tiles[S_FIRST:]:
+                for j in range(UNITS[i])[S_FIRST:]:
                     regroup(nc.scalar.copy, flipped[i][j], unit_grouped[:, j])
             if i + 1 < count:
                 flipped[i + 1] = [transpose_rows(x_rows[i + 1][:, j, :]) for j in range(UNITS[i + 1])]
             if fresh:
-                total[i - 2] = scalar_sums(q[i - 2], scalar_squares(i - 2))
-                if scalar_squares(i - 2) < UNITS[i - 2]:
-                    mean_part[i - 2] = squared_means(stats[i - 2], UNITS[i - 2], scalar_squares(i - 2))
-            if done:
-                normalise(i - 3, q[i - 3], rstd, 0, H * UNITS[i - 3])
-                if i - 3 == count - 1 or group_of[i - 2] != group_of[i - 3]:
-                    store(group_of[i - 3])
+                b = batch_of[i - 2]
+                scalar_sums(i - 2, q[i - 2], total[b])
+                if i - 2 == batch_firsts[b] + BATCHES[b] - 1 and scalar_squares(b) < tiles_in[b]:
+                    mean_part[b] = squared_means(stats[b], b)
+            for u in scaled:
+                normalise(u, q[u], rstd[batch_of[u]])
+                if u == count - 1 or group_of[u + 1] != group_of[u]:
+                    store(group_of[u])

@@ -215,17 +215,15 @@ def tile_combcrossattention_pa_t_kernel(tc, hidden_states, Wq, q_norm_w, out):
                 regroup(nc.vector.tensor_copy, w_flipped, w_grouped[:, 0])
             if i == 1:
                 quantise(w_grouped, w_codes, w_scales, 0, 1)
+            for b in closing:
+                if scalar_squares(b) < tiles_in[b]:
+                    vector_sums(stats[b], mean_part[b], total[b], b)
             n = UNITS[i - 1] if 0 <= i - 1 < count else 0
             if n:
                 codes = mx_pool.tile([P, n * PASSES * P], U32, align_bytes=64)
                 scales = mx_pool.tile([P, n * PASSES * P], U8, align_bytes=64)
                 x_mx[i - 1] = codes, scales
                 quantise(grouped[i - 1], codes, scales, 0, min(n, 2))
-            for b in closing:
-                if scalar_squares(b) < tiles_in[b]:
-                    vector_sums(stats[b], mean_part[b], total[b], b)
-            if n > 2:
-                quantise(grouped[i - 1], codes, scales, 2, n)
             if fresh:
                 b = batch_of[i - 2]
                 if i - 2 == batch_firsts[b]:
@@ -234,6 +232,8 @@ def tile_combcrossattention_pa_t_kernel(tc, hidden_states, Wq, q_norm_w, out):
                     batch_total = stat_pool.tile([P, most, H], F32)
                     total[b] = batch_total
                 statistics(i - 2, q[i - 2], stats[b])
+            if n > 2:
+                quantise(grouped[i - 1], codes, scales, 2, n)
             for b in closing:
                 rstd[b] = inverse_root(total[b], b)
             if this:

@@ -152,6 +152,11 @@ def tile_combcrossattention_pa_t_kernel(tc, hidden_states, Wq, q_norm_w, out):
                         op1=ALU.mult,
                     )
 
+        def spread_gain():
+            q = q_psum.tile([P, 4, H * D], F32)
+            nc.tensor.matmul(q[:, 0, :D], lhsT=ones[:], rhs=gain_row[:], start=True, stop=True)
+            nc.vector.tensor_copy(out=gain[:], in_=q[:, 0, :D])
+
         def store(g):
             rows = slice(group_firsts[g] * P, (group_firsts[g] + group_sizes[g]) * P)
             nc.sync.dma_start(
@@ -165,8 +170,12 @@ def tile_combcrossattention_pa_t_kernel(tc, hidden_states, Wq, q_norm_w, out):
         nc.vector.memset(eps[:], EPS)
         first_use = const.tile([P, 1], F32)
         nc.scalar.activation(out=first_use[:], in_=eps[:], func=ACT.Abs_reciprocal_sqrt)
-        gain = const.tile([P, D], BF16)
-        nc.scalar.dma_start(out=gain[:], in_=q_norm_w.partition_broadcast(P))
+        gain_row = const.tile([P, D], BF16)
+        nc.vector.memset(gain_row[:], 0.0)
+        nc.scalar.dma_start(out=gain_row[:1, :], in_=q_norm_w.unsqueeze(0))
+        ones = const.tile([P, P], BF16)
+        nc.vector.memset(ones[:], 1.0)
+        gain = const.tile([P, D], F32)
 
         w_rows = const.tile([P, E], BF16)
         x_rows = []
@@ -187,6 +196,7 @@ def tile_combcrossattention_pa_t_kernel(tc, hidden_states, Wq, q_norm_w, out):
         x_mx = {}
         q = {}
         flipped[0] = [transpose_rows(x_rows[0][:, 0, :])]
+        spread_gain()
         w_flipped = transpose_rows(w_rows[:])
         w_codes = const.tile([P, PASSES * P], U32, align_bytes=64)
         w_scales = const.tile([P, PASSES * P], U8, align_bytes=64)

import math
from contextlib import ExitStack

import concourse.mybir as mybir
from concourse.masks import make_identity

F32 = mybir.dt.float32
BF16 = mybir.dt.bfloat16
U32 = mybir.dt.uint32
U8 = mybir.dt.uint8
FP8X4 = mybir.dt.float8_e4m3fn_x4
ACT = mybir.ActivationFunctionType
ALU = mybir.AluOpType

T, E, H, D = 8192, 1024, 2, 64
EPS = 1e-05
FLOPS = 2 * T * E * H * D

P = 128
PACK = 4
K_PASS = P * PACK
PASSES = E // K_PASS
HALVES = 2
GROUPS = ((1, 3),) + 4 * ((3, 3, 3, 3),) + ((3, 3), (3,), (2,), (1,))
UNITS = tuple(n for group in GROUPS for n in group)
BATCHES = (1, 1, 1) + 8 * (2,) + 4 * (1,)
S_FIRST = 2
STATS = 6


def tile_combcrossattention_pa_t_kernel(tc, hidden_states, Wq, q_norm_w, out):
    nc = tc.nc
    firsts = [sum(UNITS[:i]) for i in range(len(UNITS))]
    count = len(UNITS)
    group_of = [g for g, group in enumerate(GROUPS) for n in group]
    group_sizes = [sum(group) for group in GROUPS]
    group_firsts = [sum(group_sizes[:g]) for g in range(len(GROUPS))]

    batch_of = [b for b, n in enumerate(BATCHES) for u in range(n)]
    batch_firsts = [sum(BATCHES[:b]) for b in range(len(BATCHES))]
    tiles_in = [sum(UNITS[f : f + n]) for f, n in zip(batch_firsts, BATCHES)]
    offset = [firsts[i] - firsts[batch_firsts[batch_of[i]]] for i in range(count)]
    scaling_round = [batch_firsts[b] + BATCHES[b] - 1 + 3 + u for b in range(len(BATCHES)) for u in range(BATCHES[b])]
    most = max(tiles_in)

    with ExitStack() as ctx:
        const = ctx.enter_context(tc.tile_pool(name="const", bufs=1))
        resident = ctx.enter_context(tc.tile_pool(name="resident", bufs=1))
        group_pool = ctx.enter_context(tc.tile_pool(name="group", bufs=3))
        mx_pool = ctx.enter_context(tc.tile_pool(name="mx", bufs=3))
        stat_pool = ctx.enter_context(tc.tile_pool(name="stat", bufs=3))
        flip_psum = ctx.enter_context(tc.psum_pool(name="flip", bufs=4))
        q_psum = ctx.enter_context(tc.psum_pool(name="q", bufs=4))
        ctx.enter_context(tc.manual_schedule())

        def scalar_squares(b):
            if b >= len(BATCHES) - 4:
                return tiles_in[b]
            return 1 if BATCHES[b] == 2 else 0

        def transpose_rows(rows):
            words = rows.bitcast(F32)
            flipped = flip_psum.tile([P, PASSES, HALVES, P], F32)
            for g in range(PASSES):
                for u in range(HALVES):
                    first = (g * HALVES + u) * P
                    nc.tensor.transpose(flipped[:, g, u, :], words[:, first : first + P], ident[:])
            return flipped

        def regroup(copy, flipped, grouped):
            copy(out=grouped.bitcast(F32), in_=flipped[:].rearrange("p g u r -> p g r u"))

        def quantise(grouped, codes, scales, first, last):
            words = slice(first * PASSES * P, last * PASSES * P)
            nc.vector.quantize_mx(
                out=codes[:, words].bitcast(FP8X4),
                scales=scales[:, words],
                in_=grouped[:, first:last].rearrange("p j g r e -> p (j g r e)"),
            )

        def project(x_mx, n):
            q = q_psum.tile([P, 4, H * D], F32)
            codes, scales = x_mx
            for j in range(n):
                for g in range(PASSES):
                    cols = slice((j * PASSES + g) * P, (j * PASSES + g + 1) * P)
                    w_cols = slice(g * P, (g + 1) * P)
                    nc.tensor.matmul_mx(
                        out=q[:, j, :],
                        lhsT=codes[:, cols].bitcast(FP8X4),
                        lhsT_scale=scales[:, cols],
                        rhs=w_codes[:, w_cols].bitcast(FP8X4),
                        rhs_scale=w_scales[:, w_cols],
                        start=(g == 0),
                        stop=(g == PASSES - 1),
                    )
            return q

        def statistics(i, q, stats):
            b = batch_of[i]
            for j in range(UNITS[i]):
                if offset[i] + j >= scalar_squares(b):
                    nc.vector.bn_stats(out=stats[:, offset[i] + j, :], in_=q[:, j, :].rearrange("p (h d) -> p d h", h=H))

        def scalar_sums(i, q, total):
            b = batch_of[i]
            squares = stat_pool.tile([P, 4, H, D], F32)
            for j in range(UNITS[i]):
                if offset[i] + j < scalar_squares(b):
                    for h in range(H):
                        nc.scalar.activation(
                            out=squares[:, j, h, :],
                            in_=q[:, j, h * D : (h + 1) * D],
                            func=ACT.Square,
                            accum_out=total[:, offset[i] + j, h : h + 1],
                        )

        def squared_means(stats, b):
            m, n = scalar_squares(b), tiles_in[b]
            mean_part = stat_pool.tile([P, most, H], F32)
            nc.scalar.activation(
                out=mean_part[:, m:n, :], in_=stats[:, m:n, 1::3], func=ACT.Square, scale=math.sqrt(D)
            )
            return mean_part

        def vector_sums(stats, mean_part, total, b):
            m, n = scalar_squares(b), tiles_in[b]
            nc.vector.tensor_add(out=total[:, m:n, :], in0=stats[:, m:n, 2::3], in1=mean_part[:, m:n, :])

        def inverse_root(total, b):
            n = tiles_in[b]
            rstd = stat_pool.tile([P, most, H], F32)
            nc.scalar.activation(
                out=rstd[:, :n, :],
                in_=total[:, :n, :],
                func=ACT.Abs_reciprocal_sqrt,
                bias=eps[:],
                scale=1.0 / D,
            )
            return rstd

        def normalise(i, q, rstd):
            g = group_of[i]
            for h in range(H):
                for j in range(UNITS[i]):
                    nc.vector.scalar_tensor_tensor(
                        out=normed[g][:, h, firsts[i] - group_firsts[g] + j, :],
                        in0=q[:, j, h * D : (h + 1) * D],
                        scalar=rstd[:, offset[i] + j, h : h + 1],
                        in1=gain[:],
                        op0=ALU.mult,
                        op1=ALU.mult,
                    )

        def spread_gain():
            q = q_psum.tile([P, 4, H * D], F32)
            nc.tensor.matmul(q[:, 0, :D], lhsT=ones[:], rhs=gain_row[:], start=True, stop=True)
            nc.vector.tensor_copy(out=gain[:], in_=q[:, 0, :D])

        def store(g):
            rows = slice(group_firsts[g] * P, (group_firsts[g] + group_sizes[g]) * P)
            nc.sync.dma_start(
                out=out[:, rows, :].rearrange("h (p j) d -> p h (j d)", j=group_sizes[g]),
                in_=normed[g][:].rearrange("p h j d -> p h (j d)"),
            )

        ident = const.tile([P, P], F32)
        make_identity(nc, ident[:])
        eps = const.tile([P, 1], F32)
        nc.vector.memset(eps[:], EPS)
        first_use = const.tile([P, 1], F32)
        nc.scalar.activation(out=first_use[:], in_=eps[:], func=ACT.Abs_reciprocal_sqrt)
        gain_row = const.tile([P, D], BF16)
        nc.vector.memset(gain_row[:], 0.0)
        nc.scalar.dma_start(out=gain_row[:1, :], in_=q_norm_w.unsqueeze(0))
        ones = const.tile([P, P], BF16)
        nc.vector.memset(ones[:], 1.0)
        gain = const.tile([P, D], F32)

        w_rows = const.tile([P, E], BF16)
        x_rows = []
        for i in range(count):
            n = UNITS[i]
            x_unit = resident.tile([P, n, E], BF16, name="x%d" % i)
            g = group_of[i]
            rows = slice(group_firsts[g] * P, (group_firsts[g] + group_sizes[g]) * P)
            x_group = hidden_states[rows, :].rearrange("(p j) k -> p j k", j=group_sizes[g])
            j = firsts[i] - group_firsts[g]
            nc.sync.dma_start(out=x_unit[:], in_=x_group[:, j : j + n])
            x_rows.append(x_unit)
            if i == 0:
                nc.sync.dma_start(out=w_rows[:], in_=Wq)

        flipped = {}
        grouped = {}
        x_mx = {}
        q = {}
        flipped[0] = [transpose_rows(x_rows[0][:, 0, :])]
        spread_gain()
        w_flipped = transpose_rows(w_rows[:])
        w_codes = const.tile([P, PASSES * P], U32, align_bytes=64)
        w_scales = const.tile([P, PASSES * P], U8, align_bytes=64)
        w_grouped = const.tile([P, 1, PASSES, P, PACK], BF16, align_bytes=64)

        total = {}
        stats = {}
        mean_part = {}
        rstd = {}
        normed = []
        for g in range(len(GROUPS)):
            normed_group = resident.tile([P, H, group_sizes[g], D], F32, name="normed%d" % g)
            normed.append(normed_group)
        for i in range(count + 3):
            this, fresh = i < count, 0 <= i - 2 < count
            closing = [b for b in range(len(BATCHES)) if batch_firsts[b] + BATCHES[b] - 1 == i - 3]
            scaled = [u for u in range(count) if scaling_round[u] == i]
            if fresh:
                q[i - 2] = project(x_mx[i - 2], UNITS[i - 2])
            if this:
                unit_grouped = group_pool.tile([P, UNITS[i], PASSES, P, PACK], BF16, align_bytes=64)
                grouped[i] = unit_grouped
                for j in range(UNITS[i])[:S_FIRST]:
                    regroup(nc.scalar.copy, flipped[i][j], unit_grouped[:, j])
            if i == 0:
                regroup(nc.vector.tensor_copy, w_flipped, w_grouped[:, 0])
            if i == 1:
                quantise(w_grouped, w_codes, w_scales, 0, 1)
            for b in closing:
                if scalar_squares(b) < tiles_in[b]:
                    vector_sums(stats[b], mean_part[b], total[b], b)
            n = UNITS[i - 1] if 0 <= i - 1 < count else 0
            if n:
                codes = mx_pool.tile([P, n * PASSES * P], U32, align_bytes=64)
                scales = mx_pool.tile([P, n * PASSES * P], U8, align_bytes=64)
                x_mx[i - 1] = codes, scales
                quantise(grouped[i - 1], codes, scales, 0, min(n, 2))
            if fresh:
                b = batch_of[i - 2]
                if i - 2 == batch_firsts[b]:
                    batch_stats = stat_pool.tile([P, most, STATS], F32)
                    stats[b] = batch_stats
                    batch_total = stat_pool.tile([P, most, H], F32)
                    total[b] = batch_total
                statistics(i - 2, q[i - 2], stats[b])
            if n > 2:
                quantise(grouped[i - 1], codes, scales, 2, n)
            for b in closing:
                rstd[b] = inverse_root(total[b], b)
            if this:
                for j in range(UNITS[i])[S_FIRST:]:
                    regroup(nc.scalar.copy, flipped[i][j], unit_grouped[:, j])
            if i + 1 < count:
                flipped[i + 1] = [transpose_rows(x_rows[i + 1][:, j, :]) for j in range(UNITS[i + 1])]
            if fresh:
                b = batch_of[i - 2]
                scalar_sums(i - 2, q[i - 2], total[b])
                if i - 2 == batch_firsts[b] + BATCHES[b] - 1 and scalar_squares(b) < tiles_in[b]:
                    mean_part[b] = squared_means(stats[b], b)
            for u in scaled:
                normalise(u, q[u], rstd[batch_of[u]])
                if u == count - 1 or group_of[u + 1] != group_of[u]:
                    store(group_of[u])
